import numpy as np
import ml_dtypes

BF16 = ml_dtypes.bfloat16


def bf(x):
    return np.asarray(x, np.float32).astype(BF16)


def f32(x):
    return np.asarray(x, np.float32)


def f64(x):
    return np.asarray(x).astype(np.float64)


def striped(idx):
    return np.tile(idx.reshape(-1, 16).T, (8, 1))


C, S, K, N = 128, 4096, 2, 8192
DIV_DIM = 10000.0


def build_pe():
    pos = np.arange(S)[None, :]
    div = np.exp(np.arange(0, C, 2) * (-(np.log(DIV_DIM) / C)))[:, None]
    pe = np.zeros((C, S))
    pe[0::2] = np.sin(div * pos)
    pe[1::2] = np.cos(div * pos)
    return pe


def setup_inputs():
    return {"pe": f32(build_pe()), "x": f32(np.random.standard_normal((C, N))), "offs": striped(np.concatenate([np.random.permutation(S) for _ in range(K)]))}


def reference(pe, x, offs):
    idx = offs[:16].T.reshape(-1)
    return f64(pe)[:, idx] + f64(x)

@@ -1,0 +1,35 @@
+import concourse.mybir as mybir
+
+F32 = mybir.dt.float32
+U16 = mybir.dt.uint16
+ADD = mybir.AluOpType.add
+
+CHANNELS = 128
+TIMES = 4096
+FRAMES = 8192
+PIECE = 1024
+PER_COLUMN = 16
+
+
+def tile_positionalencodingframe_kernel(tc, pe, x, offs, out):
+    nc = tc.nc
+    n_pieces = FRAMES // PIECE
+    with (
+        tc.tile_pool(name="held", bufs=1) as held,
+        tc.tile_pool(name="stream", bufs=n_pieces) as stream,
+    ):
+        offsets = held.tile([CHANNELS, FRAMES // PER_COLUMN], U16, name="offsets")
+        nc.sync.dma_start(offsets[:], offs)
+        table = held.tile([CHANNELS, TIMES], F32, name="table")
+        nc.sync.dma_start(table[:], pe)
+
+        for p in range(n_pieces):
+            columns = slice(p * PIECE, (p + 1) * PIECE)
+            frames = stream.tile([CHANNELS, PIECE], F32, name="frames")
+            nc.sync.dma_start(frames[:], x[:, columns])
+
+            piece_offsets = offsets[:, p * PIECE // PER_COLUMN : (p + 1) * PIECE // PER_COLUMN]
+            summed = stream.tile([CHANNELS, PIECE], F32, name="summed")
+            nc.vector.tensor_tensor(summed[:], table[:].indirect(piece_offsets), frames[:], ADD)
+
+            nc.scalar.dma_start(out[:, columns], summed[:])

@@ -6,30 +6,40 @@ ADD = mybir.AluOpType.add
 
 CHANNELS = 128
 TIMES = 4096
-FRAMES = 8192
-PIECE = 1024
+SEQUENCE = 4096
+FRAMES = 2 * SEQUENCE
+SHORTEST = 256
 PER_COLUMN = 16
+
+
+def doubling_pieces(total, first):
+    sizes = [first]
+    while sum(sizes) < total:
+        sizes.append(sum(sizes))
+    assert sum(sizes) == total
+    return sizes
 
 
 def tile_positionalencodingframe_kernel(tc, pe, x, offs, out):
     nc = tc.nc
-    n_pieces = FRAMES // PIECE
-    with (
-        tc.tile_pool(name="held", bufs=1) as held,
-        tc.tile_pool(name="stream", bufs=n_pieces) as stream,
-    ):
+    growing = doubling_pieces(SEQUENCE, SHORTEST)
+    sizes = growing + list(reversed(growing))
+
+    with tc.tile_pool(name="held", bufs=1) as held:
         offsets = held.tile([CHANNELS, FRAMES // PER_COLUMN], U16, name="offsets")
         nc.sync.dma_start(offsets[:], offs)
         table = held.tile([CHANNELS, TIMES], F32, name="table")
         nc.sync.dma_start(table[:], pe)
 
-        for p in range(n_pieces):
-            columns = slice(p * PIECE, (p + 1) * PIECE)
-            frames = stream.tile([CHANNELS, PIECE], F32, name="frames")
+        start = 0
+        for p, size in enumerate(sizes):
+            columns = slice(start, start + size)
+            frames = held.tile([CHANNELS, size], F32, name=f"frames{p}")
             nc.sync.dma_start(frames[:], x[:, columns])
 
-            piece_offsets = offsets[:, p * PIECE // PER_COLUMN : (p + 1) * PIECE // PER_COLUMN]
-            summed = stream.tile([CHANNELS, PIECE], F32, name="summed")
+            piece_offsets = offsets[:, start // PER_COLUMN : (start + size) // PER_COLUMN]
+            summed = held.tile([CHANNELS, size], F32, name=f"summed{p}")
             nc.vector.tensor_tensor(summed[:], table[:].indirect(piece_offsets), frames[:], ADD)
 
             nc.scalar.dma_start(out[:, columns], summed[:])
+            start += size

@@ -24,6 +24,7 @@ def tile_positionalencodingframe_kernel(tc, pe, x, offs, out):
     nc = tc.nc
     growing = doubling_pieces(SEQUENCE, SHORTEST)
     sizes = growing + list(reversed(growing))
+    starts = [sum(sizes[:p]) for p in range(len(sizes))]
 
     with tc.tile_pool(name="held", bufs=1) as held:
         offsets = held.tile([CHANNELS, FRAMES // PER_COLUMN], U16, name="offsets")
@@ -31,15 +32,14 @@ def tile_positionalencodingframe_kernel(tc, pe, x, offs, out):
         table = held.tile([CHANNELS, TIMES], F32, name="table")
         nc.sync.dma_start(table[:], pe)
 
-        start = 0
-        for p, size in enumerate(sizes):
-            columns = slice(start, start + size)
-            frames = held.tile([CHANNELS, size], F32, name=f"frames{p}")
-            nc.sync.dma_start(frames[:], x[:, columns])
+        frames = []
+        for p, (start, size) in enumerate(zip(starts, sizes)):
+            frames.append(held.tile([CHANNELS, size], F32, name=f"frames{p}"))
+            nc.sync.dma_start(frames[p][:], x[:, start : start + size])
 
+        for p, (start, size) in enumerate(zip(starts, sizes)):
             piece_offsets = offsets[:, start // PER_COLUMN : (start + size) // PER_COLUMN]
             summed = held.tile([CHANNELS, size], F32, name=f"summed{p}")
-            nc.vector.tensor_tensor(summed[:], table[:].indirect(piece_offsets), frames[:], ADD)
+            nc.vector.tensor_tensor(summed[:], table[:].indirect(piece_offsets), frames[p][:], ADD)
 
-            nc.scalar.dma_start(out[:, columns], summed[:])
-            start += size
+            nc.sync.dma_start(out[:, start : start + size], summed[:])

@@ -30,12 +30,13 @@ def tile_positionalencodingframe_kernel(tc, pe, x, offs, out):
         offsets = held.tile([CHANNELS, FRAMES // PER_COLUMN], U16, name="offsets")
         nc.sync.dma_start(offsets[:], offs)
         table = held.tile([CHANNELS, TIMES], F32, name="table")
-        nc.sync.dma_start(table[:], pe)
 
         frames = []
         for p, (start, size) in enumerate(zip(starts, sizes)):
             frames.append(held.tile([CHANNELS, size], F32, name=f"frames{p}"))
             nc.sync.dma_start(frames[p][:], x[:, start : start + size])
+            if p == 0:
+                nc.sync.dma_start(table[:], pe)
 
         for p, (start, size) in enumerate(zip(starts, sizes)):
             piece_offsets = offsets[:, start // PER_COLUMN : (start + size) // PER_COLUMN]

@@ -23,24 +23,38 @@ def doubling_pieces(total, first):
 def tile_positionalencodingframe_kernel(tc, pe, x, offs, out):
     nc = tc.nc
     growing = doubling_pieces(SEQUENCE, SHORTEST)
-    sizes = growing + list(reversed(growing))
-    starts = [sum(sizes[:p]) for p in range(len(sizes))]
+    starts = [sum(growing[:p]) for p in range(len(growing))]
+    shrinking = list(reversed(growing))
+    late_starts = [sum(shrinking[:p]) for p in range(len(shrinking))]
 
     with tc.tile_pool(name="held", bufs=1) as held:
         offsets = held.tile([CHANNELS, FRAMES // PER_COLUMN], U16, name="offsets")
         nc.sync.dma_start(offsets[:], offs)
         table = held.tile([CHANNELS, TIMES], F32, name="table")
 
-        frames = []
-        for p, (start, size) in enumerate(zip(starts, sizes)):
-            frames.append(held.tile([CHANNELS, size], F32, name=f"frames{p}"))
-            nc.sync.dma_start(frames[p][:], x[:, start : start + size])
+        frames = held.tile([CHANNELS, FRAMES], F32, name="frames")
+        for p, (start, size) in enumerate(zip(starts, growing)):
+            nc.sync.dma_start(frames[:, start : start + size], x[:, start : start + size])
             if p == 0:
                 nc.sync.dma_start(table[:], pe)
+        nc.sync.dma_start(frames[:, SEQUENCE:FRAMES], x[:, SEQUENCE:FRAMES])
 
-        for p, (start, size) in enumerate(zip(starts, sizes)):
+        summed = held.tile([CHANNELS, FRAMES], F32, name="summed")
+
+        def look_up_and_add(start, size):
             piece_offsets = offsets[:, start // PER_COLUMN : (start + size) // PER_COLUMN]
-            summed = held.tile([CHANNELS, size], F32, name=f"summed{p}")
-            nc.vector.tensor_tensor(summed[:], table[:].indirect(piece_offsets), frames[p][:], ADD)
+            nc.vector.tensor_tensor(
+                summed[:, start : start + size],
+                table[:].indirect(piece_offsets),
+                frames[:, start : start + size],
+                ADD,
+            )
 
-            nc.sync.dma_start(out[:, start : start + size], summed[:])
+        for start, size in zip(starts, growing):
+            look_up_and_add(start, size)
+        nc.sync.dma_start(out[:, 0:SEQUENCE], summed[:, 0:SEQUENCE])
+
+        for late_start, size in zip(late_starts, shrinking):
+            start = SEQUENCE + late_start
+            look_up_and_add(start, size)
+            nc.sync.dma_start(out[:, start : start + size], summed[:, start : start + size])

@@ -8,21 +8,24 @@ CHANNELS = 128
 TIMES = 4096
 SEQUENCE = 4096
 FRAMES = 2 * SEQUENCE
-SHORTEST = 256
 PER_COLUMN = 16
+GRAIN = 2 * PER_COLUMN
+LONGEST = SEQUENCE // 2
+SHORTER = 4
 
 
-def doubling_pieces(total, first):
-    sizes = [first]
-    while sum(sizes) < total:
-        sizes.append(sum(sizes))
-    assert sum(sizes) == total
+def doubling_pieces(total, count):
+    doubled = 2**count - 1
+    first = -(-total // (doubled * GRAIN)) * GRAIN
+    sizes = [first * 2**k for k in range(count - 1)]
+    sizes.append(total - sum(sizes))
+    assert sizes[-2] <= sizes[-1] <= 2 * sizes[-2]
     return sizes
 
 
 def tile_positionalencodingframe_kernel(tc, pe, x, offs, out):
     nc = tc.nc
-    growing = doubling_pieces(SEQUENCE, SHORTEST)
+    growing = doubling_pieces(SEQUENCE - LONGEST, SHORTER) + [LONGEST]
     starts = [sum(growing[:p]) for p in range(len(growing))]
     shrinking = list(reversed(growing))
     late_starts = [sum(shrinking[:p]) for p in range(len(shrinking))]

@@ -40,7 +40,8 @@ def tile_positionalencodingframe_kernel(tc, pe, x, offs, out):
             nc.sync.dma_start(frames[:, start : start + size], x[:, start : start + size])
             if p == 0:
                 nc.sync.dma_start(table[:], pe)
-        nc.sync.dma_start(frames[:, SEQUENCE:FRAMES], x[:, SEQUENCE:FRAMES])
+        for start in (SEQUENCE, SEQUENCE + LONGEST):
+            nc.sync.dma_start(frames[:, start : start + LONGEST], x[:, start : start + LONGEST])
 
         summed = held.tile([CHANNELS, FRAMES], F32, name="summed")
 
@@ -55,7 +56,11 @@ def tile_positionalencodingframe_kernel(tc, pe, x, offs, out):
 
         for start, size in zip(starts, growing):
             look_up_and_add(start, size)
-        nc.sync.dma_start(out[:, 0:SEQUENCE], summed[:, 0:SEQUENCE])
+            if start + size in (SEQUENCE - LONGEST, SEQUENCE):
+                nc.sync.dma_start(
+                    out[:, start + size - LONGEST : start + size],
+                    summed[:, start + size - LONGEST : start + size],
+                )
 
         for late_start, size in zip(late_starts, shrinking):
             start = SEQUENCE + late_start

@@ -12,22 +12,22 @@ PER_COLUMN = 16
 GRAIN = 2 * PER_COLUMN
 LONGEST = SEQUENCE // 2
 SHORTER = 4
+FIRST_PIECE = 128
+LAST_PIECE = 160
 
 
-def doubling_pieces(total, count):
-    doubled = 2**count - 1
-    first = -(-total // (doubled * GRAIN)) * GRAIN
+def doubling_pieces(total, count, first):
     sizes = [first * 2**k for k in range(count - 1)]
     sizes.append(total - sum(sizes))
-    assert sizes[-2] <= sizes[-1] <= 2 * sizes[-2]
+    assert first % GRAIN == 0 and sizes[-2] <= sizes[-1]
     return sizes
 
 
 def tile_positionalencodingframe_kernel(tc, pe, x, offs, out):
     nc = tc.nc
-    growing = doubling_pieces(SEQUENCE - LONGEST, SHORTER) + [LONGEST]
+    growing = doubling_pieces(SEQUENCE - LONGEST, SHORTER, FIRST_PIECE) + [LONGEST]
     starts = [sum(growing[:p]) for p in range(len(growing))]
-    shrinking = list(reversed(growing))
+    shrinking = list(reversed(doubling_pieces(SEQUENCE - LONGEST, SHORTER, LAST_PIECE) + [LONGEST]))
     late_starts = [sum(shrinking[:p]) for p in range(len(shrinking))]
 
     with tc.tile_pool(name="held", bufs=1) as held:

import concourse.mybir as mybir

F32 = mybir.dt.float32
U16 = mybir.dt.uint16
ADD = mybir.AluOpType.add

CHANNELS = 128
TIMES = 4096
SEQUENCE = 4096
FRAMES = 2 * SEQUENCE
PER_COLUMN = 16
GRAIN = 2 * PER_COLUMN
LONGEST = SEQUENCE // 2
SHORTER = 4
FIRST_PIECE = 128
LAST_PIECE = 160


def doubling_pieces(total, count, first):
    sizes = [first * 2**k for k in range(count - 1)]
    sizes.append(total - sum(sizes))
    assert first % GRAIN == 0 and sizes[-2] <= sizes[-1]
    return sizes


def tile_positionalencodingframe_kernel(tc, pe, x, offs, out):
    nc = tc.nc
    growing = doubling_pieces(SEQUENCE - LONGEST, SHORTER, FIRST_PIECE) + [LONGEST]
    starts = [sum(growing[:p]) for p in range(len(growing))]
    shrinking = list(reversed(doubling_pieces(SEQUENCE - LONGEST, SHORTER, LAST_PIECE) + [LONGEST]))
    late_starts = [sum(shrinking[:p]) for p in range(len(shrinking))]

    with tc.tile_pool(name="held", bufs=1) as held:
        offsets = held.tile([CHANNELS, FRAMES // PER_COLUMN], U16, name="offsets")
        nc.sync.dma_start(offsets[:], offs)
        table = held.tile([CHANNELS, TIMES], F32, name="table")

        frames = held.tile([CHANNELS, FRAMES], F32, name="frames")
        for p, (start, size) in enumerate(zip(starts, growing)):
            nc.sync.dma_start(frames[:, start : start + size], x[:, start : start + size])
            if p == 0:
                nc.sync.dma_start(table[:], pe)
        for start in (SEQUENCE, SEQUENCE + LONGEST):
            nc.sync.dma_start(frames[:, start : start + LONGEST], x[:, start : start + LONGEST])

        summed = held.tile([CHANNELS, FRAMES], F32, name="summed")

        def look_up_and_add(start, size):
            piece_offsets = offsets[:, start // PER_COLUMN : (start + size) // PER_COLUMN]
            nc.vector.tensor_tensor(
                summed[:, start : start + size],
                table[:].indirect(piece_offsets),
                frames[:, start : start + size],
                ADD,
            )

        for start, size in zip(starts, growing):
            look_up_and_add(start, size)
            if start + size in (SEQUENCE - LONGEST, SEQUENCE):
                nc.sync.dma_start(
                    out[:, start + size - LONGEST : start + size],
                    summed[:, start + size - LONGEST : start + size],
                )

        for late_start, size in zip(late_starts, shrinking):
            start = SEQUENCE + late_start
            look_up_and_add(start, size)
            nc.sync.dma_start(out[:, start : start + size], summed[:, start : start + size])
